import numpy as np
import ml_dtypes


def mxq(x, axis, fmt="e4m3"):
    dtype, down = {"e4m3": (ml_dtypes.float8_e4m3fn, 7), "e5m2": (ml_dtypes.float8_e5m2, 14)}[fmt]
    v = np.moveaxis(np.asarray(x, np.float32).astype(ml_dtypes.bfloat16).astype(np.float64), axis, -1)
    blocks = v.reshape(v.shape[:-1] + (-1, 32))
    amax = np.abs(blocks).max(-1, keepdims=True)
    byte = np.maximum(np.where(amax > 0, np.frexp(amax)[1] - 1 + 127, 0) - down, 1)
    scale = np.exp2(byte - 127.0)
    codes = (blocks / scale).astype(np.float32).astype(dtype).astype(np.float64)
    return np.moveaxis((codes * scale).reshape(v.shape), -1, axis)


WIDE = False


def mx_kscale(k):
    if not WIDE:
        return np.ones(k)
    levels = np.array([10, -10, 5, -5, 0])
    if k % 512:
        return np.exp2(np.random.permutation(np.resize(levels, k // 32))).repeat(32)
    a = np.empty((k // 512, 16))
    for p in range(k // 512):
        a[p, :8] = np.random.permutation(np.resize(levels, 8))
        for g in range(8):
            far = levels[np.abs(levels - a[p, g]) >= 10]
            a[p, g + 8] = far[np.random.randint(len(far))]
    return np.exp2(a.ravel()).repeat(32)


BF16 = ml_dtypes.bfloat16


def bf(x):
    return np.asarray(x, np.float32).astype(BF16)


def f64(x):
    return np.asarray(x).astype(np.float64)


N, I, O = 8192, 512, 128


def setup_inputs():
    s = mx_kscale(I)
    mask = np.tile(np.array([0.0, 0.0, 1.0, 1.0]), I // 4)
    gd = mask + 0.1 * (1.0 - mask)
    gs = (1.0 - mask) + 0.1 * mask
    x = np.random.standard_normal((N, I)) * s
    wd = np.random.standard_normal((O, I)) * gd / np.sqrt(I) / s
    ws = np.random.standard_normal((O, I)) * gs / np.sqrt(I) / s
    return {"x": bf(x), "W_dense": bf(wd), "W_sparse": bf(ws)}


def reference(x, W_dense, W_sparse):
    xq = mxq(f64(x), 1, "e4m3")
    out_dense = xq @ mxq(f64(W_dense), 1, "e4m3").T
    out_sparse = xq @ mxq(f64(W_sparse), 1, "e4m3").T
    return out_dense + out_sparse

@@ -1,0 +1,131 @@
+from contextlib import ExitStack
+
+import concourse.mybir as mybir
+from concourse.masks import make_identity
+
+F32 = mybir.dt.float32
+BF16 = mybir.dt.bfloat16
+U32 = mybir.dt.uint32
+U8 = mybir.dt.uint8
+FP8X4 = mybir.dt.float8_e4m3fn_x4
+
+P = 128
+N_ROWS, K, OUTS = 8192, 512, 128
+TILES = N_ROWS // P
+WORDS = K // 2
+FLOPS = 2 * 2 * N_ROWS * K * OUTS
+
+ROUNDS = [2, 2, 4, 8, 8, 8, 8, 8, 8, 8]
+LAG = 2
+TAIL = 3
+
+
+def tile_myinterleavedmodule_t_kernel(tc, x, W_dense, W_sparse, out):
+    nc = tc.nc
+    assert sum(ROUNDS) == TILES
+    x_rows = x.rearrange("(p t) k -> p (t k)", t=TILES)
+    out_rows = out.rearrange("(p t) o -> p (t o)", t=TILES)
+    n = len(ROUNDS)
+    first = [sum(ROUNDS[:r]) for r in range(n)]
+
+    with ExitStack() as ctx:
+        const = ctx.enter_context(tc.tile_pool(name="const", bufs=1))
+        xin = ctx.enter_context(tc.tile_pool(name="xin", bufs=1))
+        gpool = ctx.enter_context(tc.tile_pool(name="gpool", bufs=3))
+        qpool = ctx.enter_context(tc.tile_pool(name="qpool", bufs=4))
+        opool = ctx.enter_context(tc.tile_pool(name="opool", bufs=1))
+        xt_pool = ctx.enter_context(tc.psum_pool(name="xtp", bufs=4))
+        acc_pool = ctx.enter_context(tc.psum_pool(name="accp", bufs=4))
+        ctx.enter_context(tc.manual_schedule())
+
+        ident = const.tile([P, P], F32, name="ident")
+        make_identity(nc, ident[:])
+
+        w_sb = const.tile([P, 2 * K], BF16, name="w_sb")
+        nc.sync.dma_start(out=w_sb[:, 0:K], in_=W_dense)
+        nc.sync.dma_start(out=w_sb[:, K : 2 * K], in_=W_sparse)
+        x_sb = []
+        for r in range(n):
+            xs = xin.tile([P, ROUNDS[r] * K], BF16, name="x%d" % r)
+            nc.sync.dma_start(out=xs[:], in_=x_rows[:, first[r] * K : (first[r] + ROUNDS[r]) * K])
+            x_sb.append(xs)
+
+        def transpose_pairs(src, tiles, grouped):
+            words = src[:].bitcast(F32)
+            g_words = grouped[:].bitcast(F32).rearrange("p (c u) -> p c u", u=2)
+            for b in range(tiles // 2):
+                xt = xt_pool.tile([P, 2, 2 * P], F32, name="xt")
+                for a in range(2):
+                    for u in range(2):
+                        row = (2 * b + a) * WORDS
+                        nc.tensor.transpose(
+                            xt[:, u, a * P : (a + 1) * P], words[:, row + u : row + WORDS : 2], ident[:]
+                        )
+                nc.scalar.copy(
+                    out=g_words[:, 2 * b * P : (2 * b + 2) * P, :],
+                    in_=xt[:].rearrange("p u c -> p c u"),
+                )
+
+        def quantise(grouped, codes, scales, c0, c1):
+            nc.vector.quantize_mx(
+                out=codes[:, c0:c1].bitcast(FP8X4),
+                scales=scales[:, c0:c1],
+                in_=grouped[:, 4 * c0 : 4 * c1],
+            )
+
+        w_g = const.tile([P, 2 * P * 4], BF16, name="w_g", align_bytes=64)
+        w_codes = const.tile([P, 2 * P], U32, name="w_codes", align_bytes=64)
+        w_scales = const.tile([P, 2 * P], U8, name="w_scales", align_bytes=64)
+        transpose_pairs(w_sb, 2, w_g)
+        quantise(w_g, w_codes, w_scales, 0, 2 * P)
+
+        operands = {}
+        for step in range(n + LAG):
+            r, m = step, step - LAG
+            halves = []
+            if r < n:
+                cols = ROUNDS[r] * P
+                grouped = gpool.tile([P, cols * 4], BF16, name="grouped", align_bytes=64)
+                codes = qpool.tile([P, cols], U32, name="codes", align_bytes=64)
+                scales = qpool.tile([P, cols], U8, name="scales", align_bytes=64)
+                transpose_pairs(x_sb[r], ROUNDS[r], grouped)
+                operands[r] = (codes, scales)
+                halves = [(c, min(c + 4 * P, cols)) for c in range(0, cols, 4 * P)]
+            banks = []
+            if m >= 0:
+                m_codes, m_scales = operands[m]
+                o_sb = opool.tile([P, ROUNDS[m] * OUTS], F32, name="o%d" % m)
+                for t0 in range(0, ROUNDS[m], 4):
+                    nt = min(4, ROUNDS[m] - t0)
+                    acc = acc_pool.tile([P, 4 * OUTS], F32, name="acc")
+                    for j in range(nt):
+                        c = (t0 + j) * P
+                        for w in range(2):
+                            nc.tensor.matmul_mx(
+                                out=acc[:, j * OUTS : (j + 1) * OUTS],
+                                lhsT=m_codes[:, c : c + P].bitcast(FP8X4),
+                                lhsT_scale=m_scales[:, c : c + P],
+                                rhs=w_codes[:, w * P : (w + 1) * P].bitcast(FP8X4),
+                                rhs_scale=w_scales[:, w * P : (w + 1) * P],
+                                start=(w == 0),
+                                stop=(w == 1),
+                            )
+                    banks.append((acc, t0, nt))
+            for i in range(max(len(halves), len(banks))):
+                if i < len(halves):
+                    quantise(grouped, codes, scales, halves[i][0], halves[i][1])
+                if i < len(banks):
+                    acc, t0, nt = banks[i]
+                    o_part = o_sb[:, t0 * OUTS : (t0 + nt) * OUTS]
+                    if m >= n - TAIL and i % 2 == 1:
+                        nc.scalar.copy(out=o_part, in_=acc[:, 0 : nt * OUTS])
+                    else:
+                        nc.vector.tensor_copy(out=o_part, in_=acc[:, 0 : nt * OUTS])
+                    if m >= n - TAIL:
+                        nc.sync.dma_start(
+                            out=out_rows[:, (first[m] + t0) * OUTS : (first[m] + t0 + nt) * OUTS], in_=o_part
+                        )
+            if 0 <= m < n - TAIL:
+                nc.sync.dma_start(
+                    out=out_rows[:, first[m] * OUTS : (first[m] + ROUNDS[m]) * OUTS], in_=o_sb[:]
+                )

@@ -15,9 +15,9 @@ TILES = N_ROWS // P
 WORDS = K // 2
 FLOPS = 2 * 2 * N_ROWS * K * OUTS
 
-ROUNDS = [2, 2, 4, 8, 8, 8, 8, 8, 8, 8]
+ROUNDS = [2, 2, 4, 8, 8, 8, 8, 8, 8, 4, 2, 2]
+DIRECT = 2
 LAG = 2
-TAIL = 3
 
 
 def tile_myinterleavedmodule_t_kernel(tc, x, W_dense, W_sparse, out):
@@ -31,6 +31,7 @@ def tile_myinterleavedmodule_t_kernel(tc, x, W_dense, W_sparse, out):
     with ExitStack() as ctx:
         const = ctx.enter_context(tc.tile_pool(name="const", bufs=1))
         xin = ctx.enter_context(tc.tile_pool(name="xin", bufs=1))
+        spool = ctx.enter_context(tc.tile_pool(name="spool", bufs=3))
         gpool = ctx.enter_context(tc.tile_pool(name="gpool", bufs=3))
         qpool = ctx.enter_context(tc.tile_pool(name="qpool", bufs=4))
         opool = ctx.enter_context(tc.tile_pool(name="opool", bufs=1))
@@ -42,25 +43,36 @@ def tile_myinterleavedmodule_t_kernel(tc, x, W_dense, W_sparse, out):
         make_identity(nc, ident[:])
 
         w_sb = const.tile([P, 2 * K], BF16, name="w_sb")
-        nc.sync.dma_start(out=w_sb[:, 0:K], in_=W_dense)
-        nc.sync.dma_start(out=w_sb[:, K : 2 * K], in_=W_sparse)
         x_sb = []
         for r in range(n):
+            if r == 2:
+                nc.sync.dma_start(out=w_sb[:, 0:K], in_=W_dense)
+                nc.sync.dma_start(out=w_sb[:, K : 2 * K], in_=W_sparse)
             xs = xin.tile([P, ROUNDS[r] * K], BF16, name="x%d" % r)
             nc.sync.dma_start(out=xs[:], in_=x_rows[:, first[r] * K : (first[r] + ROUNDS[r]) * K])
             x_sb.append(xs)
 
-        def transpose_pairs(src, tiles, grouped):
+        def split_words(r):
+            direct = strided_words(x_sb[r])
+            tiles = ROUNDS[r] - DIRECT
+            if tiles == 0:
+                return direct
+            split = spool.tile([P, 2, tiles * P], F32, name="split")
+            words = x_sb[r][:].bitcast(F32).rearrange("p (w u) -> p u w", u=2)
+            nc.vector.tensor_copy(out=split[:], in_=words[:, :, DIRECT * P :])
+            return lambda t, u: direct(t, u) if t < DIRECT else split[:, u, (t - DIRECT) * P : (t - DIRECT + 1) * P]
+
+        def strided_words(src):
             words = src[:].bitcast(F32)
+            return lambda t, u: words[:, t * WORDS + u : (t + 1) * WORDS : 2]
+
+        def transpose_pairs(half_row, tiles, grouped):
             g_words = grouped[:].bitcast(F32).rearrange("p (c u) -> p c u", u=2)
             for b in range(tiles // 2):
                 xt = xt_pool.tile([P, 2, 2 * P], F32, name="xt")
                 for a in range(2):
                     for u in range(2):
-                        row = (2 * b + a) * WORDS
-                        nc.tensor.transpose(
-                            xt[:, u, a * P : (a + 1) * P], words[:, row + u : row + WORDS : 2], ident[:]
-                        )
+                        nc.tensor.transpose(xt[:, u, a * P : (a + 1) * P], half_row(2 * b + a, u), ident[:])
                 nc.scalar.copy(
                     out=g_words[:, 2 * b * P : (2 * b + 2) * P, :],
                     in_=xt[:].rearrange("p u c -> p c u"),
@@ -76,19 +88,19 @@ def tile_myinterleavedmodule_t_kernel(tc, x, W_dense, W_sparse, out):
         w_g = const.tile([P, 2 * P * 4], BF16, name="w_g", align_bytes=64)
         w_codes = const.tile([P, 2 * P], U32, name="w_codes", align_bytes=64)
         w_scales = const.tile([P, 2 * P], U8, name="w_scales", align_bytes=64)
-        transpose_pairs(w_sb, 2, w_g)
-        quantise(w_g, w_codes, w_scales, 0, 2 * P)
-
+        half_rows = {0: split_words(0)}
         operands = {}
         for step in range(n + LAG):
             r, m = step, step - LAG
             halves = []
+            if r + 1 < n:
+                half_rows[r + 1] = split_words(r + 1)
             if r < n:
                 cols = ROUNDS[r] * P
                 grouped = gpool.tile([P, cols * 4], BF16, name="grouped", align_bytes=64)
                 codes = qpool.tile([P, cols], U32, name="codes", align_bytes=64)
                 scales = qpool.tile([P, cols], U8, name="scales", align_bytes=64)
-                transpose_pairs(x_sb[r], ROUNDS[r], grouped)
+                transpose_pairs(half_rows[r], ROUNDS[r], grouped)
                 operands[r] = (codes, scales)
                 halves = [(c, min(c + 4 * P, cols)) for c in range(0, cols, 4 * P)]
             banks = []
@@ -111,21 +123,21 @@ def tile_myinterleavedmodule_t_kernel(tc, x, W_dense, W_sparse, out):
                                 stop=(w == 1),
                             )
                     banks.append((acc, t0, nt))
+            if r == 1:
+                transpose_pairs(strided_words(w_sb), 2, w_g)
             for i in range(max(len(halves), len(banks))):
                 if i < len(halves):
                     quantise(grouped, codes, scales, halves[i][0], halves[i][1])
                 if i < len(banks):
                     acc, t0, nt = banks[i]
                     o_part = o_sb[:, t0 * OUTS : (t0 + nt) * OUTS]
-                    if m >= n - TAIL and i % 2 == 1:
+                    if i % 2 == 1:
                         nc.scalar.copy(out=o_part, in_=acc[:, 0 : nt * OUTS])
                     else:
                         nc.vector.tensor_copy(out=o_part, in_=acc[:, 0 : nt * OUTS])
-                    if m >= n - TAIL:
-                        nc.sync.dma_start(
-                            out=out_rows[:, (first[m] + t0) * OUTS : (first[m] + t0 + nt) * OUTS], in_=o_part
-                        )
-            if 0 <= m < n - TAIL:
+            if r == 1:
+                quantise(w_g, w_codes, w_scales, 0, 2 * P)
+            if m >= 0:
                 nc.sync.dma_start(
                     out=out_rows[:, first[m] * OUTS : (first[m] + ROUNDS[m]) * OUTS], in_=o_sb[:]
                 )

@@ -15,9 +15,11 @@ TILES = N_ROWS // P
 WORDS = K // 2
 FLOPS = 2 * 2 * N_ROWS * K * OUTS
 
-ROUNDS = [2, 2, 4, 8, 8, 8, 8, 8, 8, 4, 2, 2]
+ROUNDS = [2, 2, 2, 2, 4, 8, 8, 8, 8, 8, 8, 2, 2]
+FILL = 4
 DIRECT = 2
-LAG = 2
+AHEAD = 5
+W_AFTER = 1
 
 
 def tile_myinterleavedmodule_t_kernel(tc, x, W_dense, W_sparse, out):
@@ -26,14 +28,14 @@ def tile_myinterleavedmodule_t_kernel(tc, x, W_dense, W_sparse, out):
     x_rows = x.rearrange("(p t) k -> p (t k)", t=TILES)
     out_rows = out.rearrange("(p t) o -> p (t o)", t=TILES)
     n = len(ROUNDS)
-    first = [sum(ROUNDS[:r]) for r in range(n)]
+    first = [sum(ROUNDS[:r]) for r in range(n + 1)]
 
     with ExitStack() as ctx:
         const = ctx.enter_context(tc.tile_pool(name="const", bufs=1))
         xin = ctx.enter_context(tc.tile_pool(name="xin", bufs=1))
         spool = ctx.enter_context(tc.tile_pool(name="spool", bufs=3))
         gpool = ctx.enter_context(tc.tile_pool(name="gpool", bufs=3))
-        qpool = ctx.enter_context(tc.tile_pool(name="qpool", bufs=4))
+        qpool = ctx.enter_context(tc.tile_pool(name="qpool", bufs=6))
         opool = ctx.enter_context(tc.tile_pool(name="opool", bufs=1))
         xt_pool = ctx.enter_context(tc.psum_pool(name="xtp", bufs=4))
         acc_pool = ctx.enter_context(tc.psum_pool(name="accp", bufs=4))
@@ -45,35 +47,35 @@ def tile_myinterleavedmodule_t_kernel(tc, x, W_dense, W_sparse, out):
         w_sb = const.tile([P, 2 * K], BF16, name="w_sb")
         x_sb = []
         for r in range(n):
-            if r == 2:
+            if r == W_AFTER:
                 nc.sync.dma_start(out=w_sb[:, 0:K], in_=W_dense)
                 nc.sync.dma_start(out=w_sb[:, K : 2 * K], in_=W_sparse)
             xs = xin.tile([P, ROUNDS[r] * K], BF16, name="x%d" % r)
-            nc.sync.dma_start(out=xs[:], in_=x_rows[:, first[r] * K : (first[r] + ROUNDS[r]) * K])
+            nc.sync.dma_start(out=xs[:], in_=x_rows[:, first[r] * K : first[r + 1] * K])
             x_sb.append(xs)
+
+        def strided_words(src):
+            words = src[:].bitcast(F32)
+            return lambda t, u: words[:, t * WORDS + u : (t + 1) * WORDS : 2]
 
         def split_words(r):
             direct = strided_words(x_sb[r])
             tiles = ROUNDS[r] - DIRECT
-            if tiles == 0:
+            if r < FILL or tiles == 0:
                 return direct
             split = spool.tile([P, 2, tiles * P], F32, name="split")
             words = x_sb[r][:].bitcast(F32).rearrange("p (w u) -> p u w", u=2)
             nc.vector.tensor_copy(out=split[:], in_=words[:, :, DIRECT * P :])
             return lambda t, u: direct(t, u) if t < DIRECT else split[:, u, (t - DIRECT) * P : (t - DIRECT + 1) * P]
 
-        def strided_words(src):
-            words = src[:].bitcast(F32)
-            return lambda t, u: words[:, t * WORDS + u : (t + 1) * WORDS : 2]
-
-        def transpose_pairs(half_row, tiles, grouped):
+        def transpose_pairs(half_row, tiles, grouped, engines):
             g_words = grouped[:].bitcast(F32).rearrange("p (c u) -> p c u", u=2)
             for b in range(tiles // 2):
                 xt = xt_pool.tile([P, 2, 2 * P], F32, name="xt")
                 for a in range(2):
                     for u in range(2):
                         nc.tensor.transpose(xt[:, u, a * P : (a + 1) * P], half_row(2 * b + a, u), ident[:])
-                nc.scalar.copy(
+                engines[b % len(engines)](
                     out=g_words[:, 2 * b * P : (2 * b + 2) * P, :],
                     in_=xt[:].rearrange("p u c -> p c u"),
                 )
@@ -85,13 +87,17 @@ def tile_myinterleavedmodule_t_kernel(tc, x, W_dense, W_sparse, out):
                 in_=grouped[:, 4 * c0 : 4 * c1],
             )
 
+        on_vector, on_scalar = nc.vector.tensor_copy, nc.scalar.copy
         w_g = const.tile([P, 2 * P * 4], BF16, name="w_g", align_bytes=64)
         w_codes = const.tile([P, 2 * P], U32, name="w_codes", align_bytes=64)
         w_scales = const.tile([P, 2 * P], U8, name="w_scales", align_bytes=64)
+
         half_rows = {0: split_words(0)}
         operands = {}
-        for step in range(n + LAG):
-            r, m = step, step - LAG
+        m = 0
+        emptied = 0
+        r = 0
+        while m < n:
             halves = []
             if r + 1 < n:
                 half_rows[r + 1] = split_words(r + 1)
@@ -100,11 +106,13 @@ def tile_myinterleavedmodule_t_kernel(tc, x, W_dense, W_sparse, out):
                 grouped = gpool.tile([P, cols * 4], BF16, name="grouped", align_bytes=64)
                 codes = qpool.tile([P, cols], U32, name="codes", align_bytes=64)
                 scales = qpool.tile([P, cols], U8, name="scales", align_bytes=64)
-                transpose_pairs(half_rows[r], ROUNDS[r], grouped)
+                transpose_pairs(half_rows[r], ROUNDS[r], grouped, [on_vector] if r in (1, 3) else [on_scalar])
                 operands[r] = (codes, scales)
                 halves = [(c, min(c + 4 * P, cols)) for c in range(0, cols, 4 * P)]
+            if r == W_AFTER:
+                transpose_pairs(strided_words(w_sb), 2, w_g, [on_scalar])
             banks = []
-            if m >= 0:
+            while m < n and (r >= n or first[min(r + 1, n)] - first[m + 1] >= AHEAD):
                 m_codes, m_scales = operands[m]
                 o_sb = opool.tile([P, ROUNDS[m] * OUTS], F32, name="o%d" % m)
                 for t0 in range(0, ROUNDS[m], 4):
@@ -122,22 +130,22 @@ def tile_myinterleavedmodule_t_kernel(tc, x, W_dense, W_sparse, out):
                                 start=(w == 0),
                                 stop=(w == 1),
                             )
-                    banks.append((acc, t0, nt))
-            if r == 1:
-                transpose_pairs(strided_words(w_sb), 2, w_g)
+                    banks.append((m, o_sb, acc, t0, nt))
+                m += 1
+                if r >= n:
+                    break
             for i in range(max(len(halves), len(banks))):
                 if i < len(halves):
                     quantise(grouped, codes, scales, halves[i][0], halves[i][1])
+                if i == 0 and r == W_AFTER:
+                    quantise(w_g, w_codes, w_scales, 0, 2 * P)
                 if i < len(banks):
-                    acc, t0, nt = banks[i]
+                    b, o_sb, acc, t0, nt = banks[i]
+                    copy = on_vector if emptied % 2 == 0 else on_scalar
+                    emptied += 1
                     o_part = o_sb[:, t0 * OUTS : (t0 + nt) * OUTS]
-                    if i % 2 == 1:
-                        nc.scalar.copy(out=o_part, in_=acc[:, 0 : nt * OUTS])
-                    else:
-                        nc.vector.tensor_copy(out=o_part, in_=acc[:, 0 : nt * OUTS])
-            if r == 1:
-                quantise(w_g, w_codes, w_scales, 0, 2 * P)
-            if m >= 0:
-                nc.sync.dma_start(
-                    out=out_rows[:, first[m] * OUTS : (first[m] + ROUNDS[m]) * OUTS], in_=o_sb[:]
-                )
+                    copy(out=o_part, in_=acc[:, 0 : nt * OUTS])
+                    nc.sync.dma_start(
+                        out=out_rows[:, (first[b] + t0) * OUTS : (first[b] + t0 + nt) * OUTS], in_=o_part
+                    )
+            r += 1

@@ -15,10 +15,10 @@ TILES = N_ROWS // P
 WORDS = K // 2
 FLOPS = 2 * 2 * N_ROWS * K * OUTS
 
-ROUNDS = [2, 2, 2, 2, 4, 8, 8, 8, 8, 8, 8, 2, 2]
-FILL = 4
-DIRECT = 2
-AHEAD = 5
+ROUNDS = [2] * 4 + [4] * 13 + [2] * 2
+FILL = 5
+DIRECT = 1
+AHEAD = 8
 W_AFTER = 1
 
 
@@ -33,8 +33,8 @@ def tile_myinterleavedmodule_t_kernel(tc, x, W_dense, W_sparse, out):
     with ExitStack() as ctx:
         const = ctx.enter_context(tc.tile_pool(name="const", bufs=1))
         xin = ctx.enter_context(tc.tile_pool(name="xin", bufs=1))
-        spool = ctx.enter_context(tc.tile_pool(name="spool", bufs=3))
-        gpool = ctx.enter_context(tc.tile_pool(name="gpool", bufs=3))
+        spool = ctx.enter_context(tc.tile_pool(name="spool", bufs=4))
+        gpool = ctx.enter_context(tc.tile_pool(name="gpool", bufs=4))
         qpool = ctx.enter_context(tc.tile_pool(name="qpool", bufs=6))
         opool = ctx.enter_context(tc.tile_pool(name="opool", bufs=1))
         xt_pool = ctx.enter_context(tc.psum_pool(name="xtp", bufs=4))
@@ -61,21 +61,21 @@ def tile_myinterleavedmodule_t_kernel(tc, x, W_dense, W_sparse, out):
         def split_words(r):
             direct = strided_words(x_sb[r])
             tiles = ROUNDS[r] - DIRECT
-            if r < FILL or tiles == 0:
+            if r < FILL or r >= n - 2:
                 return direct
             split = spool.tile([P, 2, tiles * P], F32, name="split")
             words = x_sb[r][:].bitcast(F32).rearrange("p (w u) -> p u w", u=2)
             nc.vector.tensor_copy(out=split[:], in_=words[:, :, DIRECT * P :])
             return lambda t, u: direct(t, u) if t < DIRECT else split[:, u, (t - DIRECT) * P : (t - DIRECT + 1) * P]
 
-        def transpose_pairs(half_row, tiles, grouped, engines):
+        def transpose_pairs(half_row, tiles, grouped):
             g_words = grouped[:].bitcast(F32).rearrange("p (c u) -> p c u", u=2)
             for b in range(tiles // 2):
                 xt = xt_pool.tile([P, 2, 2 * P], F32, name="xt")
                 for a in range(2):
                     for u in range(2):
                         nc.tensor.transpose(xt[:, u, a * P : (a + 1) * P], half_row(2 * b + a, u), ident[:])
-                engines[b % len(engines)](
+                nc.scalar.copy(
                     out=g_words[:, 2 * b * P : (2 * b + 2) * P, :],
                     in_=xt[:].rearrange("p u c -> p c u"),
                 )
@@ -92,25 +92,25 @@ def tile_myinterleavedmodule_t_kernel(tc, x, W_dense, W_sparse, out):
         w_codes = const.tile([P, 2 * P], U32, name="w_codes", align_bytes=64)
         w_scales = const.tile([P, 2 * P], U8, name="w_scales", align_bytes=64)
 
-        half_rows = {0: split_words(0)}
+        half_rows = {r: split_words(r) for r in range(2)}
         operands = {}
         m = 0
         emptied = 0
         r = 0
         while m < n:
             halves = []
-            if r + 1 < n:
-                half_rows[r + 1] = split_words(r + 1)
+            if r + 2 < n:
+                half_rows[r + 2] = split_words(r + 2)
             if r < n:
                 cols = ROUNDS[r] * P
                 grouped = gpool.tile([P, cols * 4], BF16, name="grouped", align_bytes=64)
                 codes = qpool.tile([P, cols], U32, name="codes", align_bytes=64)
                 scales = qpool.tile([P, cols], U8, name="scales", align_bytes=64)
-                transpose_pairs(half_rows[r], ROUNDS[r], grouped, [on_vector] if r in (1, 3) else [on_scalar])
+                transpose_pairs(half_rows[r], ROUNDS[r], grouped)
                 operands[r] = (codes, scales)
                 halves = [(c, min(c + 4 * P, cols)) for c in range(0, cols, 4 * P)]
             if r == W_AFTER:
-                transpose_pairs(strided_words(w_sb), 2, w_g, [on_scalar])
+                transpose_pairs(strided_words(w_sb), 2, w_g)
             banks = []
             while m < n and (r >= n or first[min(r + 1, n)] - first[m + 1] >= AHEAD):
                 m_codes, m_scales = operands[m]

from contextlib import ExitStack

import concourse.mybir as mybir
from concourse.masks import make_identity

F32 = mybir.dt.float32
BF16 = mybir.dt.bfloat16
U32 = mybir.dt.uint32
U8 = mybir.dt.uint8
FP8X4 = mybir.dt.float8_e4m3fn_x4

P = 128
N_ROWS, K, OUTS = 8192, 512, 128
TILES = N_ROWS // P
WORDS = K // 2
FLOPS = 2 * 2 * N_ROWS * K * OUTS

ROUNDS = [2] * 4 + [4] * 13 + [2] * 2
FILL = 5
DIRECT = 1
AHEAD = 8
W_AFTER = 1


def tile_myinterleavedmodule_t_kernel(tc, x, W_dense, W_sparse, out):
    nc = tc.nc
    assert sum(ROUNDS) == TILES
    x_rows = x.rearrange("(p t) k -> p (t k)", t=TILES)
    out_rows = out.rearrange("(p t) o -> p (t o)", t=TILES)
    n = len(ROUNDS)
    first = [sum(ROUNDS[:r]) for r in range(n + 1)]

    with ExitStack() as ctx:
        const = ctx.enter_context(tc.tile_pool(name="const", bufs=1))
        xin = ctx.enter_context(tc.tile_pool(name="xin", bufs=1))
        spool = ctx.enter_context(tc.tile_pool(name="spool", bufs=4))
        gpool = ctx.enter_context(tc.tile_pool(name="gpool", bufs=4))
        qpool = ctx.enter_context(tc.tile_pool(name="qpool", bufs=6))
        opool = ctx.enter_context(tc.tile_pool(name="opool", bufs=1))
        xt_pool = ctx.enter_context(tc.psum_pool(name="xtp", bufs=4))
        acc_pool = ctx.enter_context(tc.psum_pool(name="accp", bufs=4))
        ctx.enter_context(tc.manual_schedule())

        ident = const.tile([P, P], F32, name="ident")
        make_identity(nc, ident[:])

        w_sb = const.tile([P, 2 * K], BF16, name="w_sb")
        x_sb = []
        for r in range(n):
            if r == W_AFTER:
                nc.sync.dma_start(out=w_sb[:, 0:K], in_=W_dense)
                nc.sync.dma_start(out=w_sb[:, K : 2 * K], in_=W_sparse)
            xs = xin.tile([P, ROUNDS[r] * K], BF16, name="x%d" % r)
            nc.sync.dma_start(out=xs[:], in_=x_rows[:, first[r] * K : first[r + 1] * K])
            x_sb.append(xs)

        def strided_words(src):
            words = src[:].bitcast(F32)
            return lambda t, u: words[:, t * WORDS + u : (t + 1) * WORDS : 2]

        def split_words(r):
            direct = strided_words(x_sb[r])
            tiles = ROUNDS[r] - DIRECT
            if r < FILL or r >= n - 2:
                return direct
            split = spool.tile([P, 2, tiles * P], F32, name="split")
            words = x_sb[r][:].bitcast(F32).rearrange("p (w u) -> p u w", u=2)
            nc.vector.tensor_copy(out=split[:], in_=words[:, :, DIRECT * P :])
            return lambda t, u: direct(t, u) if t < DIRECT else split[:, u, (t - DIRECT) * P : (t - DIRECT + 1) * P]

        def transpose_pairs(half_row, tiles, grouped):
            g_words = grouped[:].bitcast(F32).rearrange("p (c u) -> p c u", u=2)
            for b in range(tiles // 2):
                xt = xt_pool.tile([P, 2, 2 * P], F32, name="xt")
                for a in range(2):
                    for u in range(2):
                        nc.tensor.transpose(xt[:, u, a * P : (a + 1) * P], half_row(2 * b + a, u), ident[:])
                nc.scalar.copy(
                    out=g_words[:, 2 * b * P : (2 * b + 2) * P, :],
                    in_=xt[:].rearrange("p u c -> p c u"),
                )

        def quantise(grouped, codes, scales, c0, c1):
            nc.vector.quantize_mx(
                out=codes[:, c0:c1].bitcast(FP8X4),
                scales=scales[:, c0:c1],
                in_=grouped[:, 4 * c0 : 4 * c1],
            )

        on_vector, on_scalar = nc.vector.tensor_copy, nc.scalar.copy
        w_g = const.tile([P, 2 * P * 4], BF16, name="w_g", align_bytes=64)
        w_codes = const.tile([P, 2 * P], U32, name="w_codes", align_bytes=64)
        w_scales = const.tile([P, 2 * P], U8, name="w_scales", align_bytes=64)

        half_rows = {r: split_words(r) for r in range(2)}
        operands = {}
        m = 0
        emptied = 0
        r = 0
        while m < n:
            halves = []
            if r + 2 < n:
                half_rows[r + 2] = split_words(r + 2)
            if r < n:
                cols = ROUNDS[r] * P
                grouped = gpool.tile([P, cols * 4], BF16, name="grouped", align_bytes=64)
                codes = qpool.tile([P, cols], U32, name="codes", align_bytes=64)
                scales = qpool.tile([P, cols], U8, name="scales", align_bytes=64)
                transpose_pairs(half_rows[r], ROUNDS[r], grouped)
                operands[r] = (codes, scales)
                halves = [(c, min(c + 4 * P, cols)) for c in range(0, cols, 4 * P)]
            if r == W_AFTER:
                transpose_pairs(strided_words(w_sb), 2, w_g)
            banks = []
            while m < n and (r >= n or first[min(r + 1, n)] - first[m + 1] >= AHEAD):
                m_codes, m_scales = operands[m]
                o_sb = opool.tile([P, ROUNDS[m] * OUTS], F32, name="o%d" % m)
                for t0 in range(0, ROUNDS[m], 4):
                    nt = min(4, ROUNDS[m] - t0)
                    acc = acc_pool.tile([P, 4 * OUTS], F32, name="acc")
                    for j in range(nt):
                        c = (t0 + j) * P
                        for w in range(2):
                            nc.tensor.matmul_mx(
                                out=acc[:, j * OUTS : (j + 1) * OUTS],
                                lhsT=m_codes[:, c : c + P].bitcast(FP8X4),
                                lhsT_scale=m_scales[:, c : c + P],
                                rhs=w_codes[:, w * P : (w + 1) * P].bitcast(FP8X4),
                                rhs_scale=w_scales[:, w * P : (w + 1) * P],
                                start=(w == 0),
                                stop=(w == 1),
                            )
                    banks.append((m, o_sb, acc, t0, nt))
                m += 1
                if r >= n:
                    break
            for i in range(max(len(halves), len(banks))):
                if i < len(halves):
                    quantise(grouped, codes, scales, halves[i][0], halves[i][1])
                if i == 0 and r == W_AFTER:
                    quantise(w_g, w_codes, w_scales, 0, 2 * P)
                if i < len(banks):
                    b, o_sb, acc, t0, nt = banks[i]
                    copy = on_vector if emptied % 2 == 0 else on_scalar
                    emptied += 1
                    o_part = o_sb[:, t0 * OUTS : (t0 + nt) * OUTS]
                    copy(out=o_part, in_=acc[:, 0 : nt * OUTS])
                    nc.sync.dma_start(
                        out=out_rows[:, (first[b] + t0) * OUTS : (first[b] + t0 + nt) * OUTS], in_=o_part
                    )
            r += 1
